import numpy as np
import ml_dtypes

BF16 = ml_dtypes.bfloat16


def bf(x):
    return np.asarray(x, np.float32).astype(BF16)


def f32(x):
    return np.asarray(x, np.float32)


def f64(x):
    return np.asarray(x).astype(np.float64)


def striped(idx):
    return np.tile(idx.reshape(-1, 16).T, (8, 1))


D, S, M, N, R = 128, 2048, 256, 1024, 16


def project_to_ball(v):
    nrm = np.sqrt(np.sum(v * v, axis=0, keepdims=True))
    return v * (0.9 / (1.0 + nrm))


def points(basis, count):
    z = basis @ np.random.standard_normal((R, count)) / np.sqrt(D * R)
    return project_to_ball(z * np.random.uniform(0.5, 6.0, (1, count)))


def setup_inputs():
    basis = np.random.standard_normal((D, R))
    return {"table": bf(points(basis, S)), "w": bf(points(basis, M)), "offs": striped(np.random.permutation(S)[:N])}


def reference(table, w, offs):
    idx = offs[:16].T.reshape(-1)
    xg = f64(table)[:, idx]
    cw = f64(w)
    x2 = np.sum(xg * xg, axis=0)[None, :]
    c2 = np.sum(cw * cw, axis=0)[:, None]
    xc = cw.T @ xg
    sqd = x2 + c2 - 2.0 * xc
    a = 1.0 + 2.0 * sqd / ((1.0 - x2) * (1.0 - c2))
    return np.log(a + np.sqrt(a * a - 1.0))

@@ -1,0 +1,104 @@
+import concourse.mybir as mybir
+from concourse.masks import make_identity
+
+P = 128
+STORE = 2048
+CENTROIDS = 256
+KEPT = 1024
+PIECE = 512
+N_PIECES = KEPT // PIECE
+N_BLOCKS = CENTROIDS // P
+TINY = 1e-30
+
+FLOPS = 2 * P * CENTROIDS * KEPT + 2 * P * KEPT + 2 * P * CENTROIDS
+BYTES = 2 * P * KEPT + 2 * P * CENTROIDS + 2 * P * (KEPT // 16) + 4 * CENTROIDS * KEPT
+
+BF16, F32, U16 = mybir.dt.bfloat16, mybir.dt.float32, mybir.dt.uint16
+ALU = mybir.AluOpType
+ACT = mybir.ActivationFunctionType
+
+
+def tile_centroiddistance_kernel(tc, table, w, offs, out):
+    nc = tc.nc
+    with (
+        tc.tile_pool(name="held", bufs=1) as held,
+        tc.tile_pool(name="work", bufs=1) as work,
+        tc.psum_pool(name="sums", bufs=1) as sums,
+        tc.psum_pool(name="picked", bufs=2) as picked,
+    ):
+        offsets = held.tile([P, KEPT // 16], U16, name="offsets")
+        nc.sync.dma_start(offsets[:], offs)
+        w_sb = held.tile([P, CENTROIDS], BF16, name="w_sb")
+        nc.scalar.dma_start(w_sb[:], w)
+        table_sb = held.tile([P, STORE], BF16, name="table_sb")
+        half = STORE // 2
+        nc.sync.dma_start(table_sb[:, :half], table[:, :half])
+        nc.scalar.dma_start(table_sb[:, half:], table[:, half:])
+
+        ident = held.tile([P, P], BF16, name="ident")
+        make_identity(nc, ident[:])
+        ones_w = held.tile([P, P], BF16, name="ones_w")
+        nc.vector.memset(ones_w[:], 1.0)
+        minus_ones_w = held.tile([P, P], BF16, name="minus_ones_w")
+        nc.vector.memset(minus_ones_w[:], -1.0)
+        ones_mv = held.tile([P, PIECE], BF16, name="ones_mv")
+        nc.gpsimd.memset(ones_mv[:], 1.0)
+        inv_p_mv = held.tile([P, PIECE], BF16, name="inv_p_mv")
+        nc.gpsimd.memset(inv_p_mv[:], 1.0 / P)
+
+        w_sq = held.tile([P, CENTROIDS], BF16, name="w_sq")
+        nc.vector.tensor_tensor(w_sq[:], w_sb[:], w_sb[:], ALU.mult)
+        w_m2 = held.tile([P, CENTROIDS], BF16, name="w_m2")
+        nc.vector.tensor_scalar(w_m2[:], w_sb[:], -2.0, None, op0=ALU.mult)
+
+        c2_ps = picked.tile([P, N_BLOCKS], F32, name="c2_ps", tag="picked")
+        for b in range(N_BLOCKS):
+            nc.tensor.matmul(
+                c2_ps[:, b : b + 1], w_sq[:, b * P : (b + 1) * P], ones_mv[:, 0:1], start=True, stop=True
+            )
+        f = held.tile([P, N_BLOCKS], F32, name="f")
+        nc.vector.tensor_scalar(f[:], c2_ps[:], -1.0, 1.0, op0=ALU.mult, op1=ALU.add)
+        s = held.tile([P, N_BLOCKS], F32, name="s")
+        nc.vector.reciprocal(s[:], f[:])
+        nc.vector.tensor_scalar(s[:], s[:], 2.0, None, op0=ALU.mult)
+
+        sqd = [[sums.tile([P, PIECE], F32, name=f"sqd{p}{b}") for b in range(N_BLOCKS)] for p in range(N_PIECES)]
+        e_ps = [sums.tile([P, PIECE], F32, name=f"e_ps{p}") for p in range(N_PIECES)]
+        for p in range(N_PIECES):
+            nc.tensor.matmul(e_ps[p][:], ones_w[:], inv_p_mv[:], start=True, stop=False)
+            for b in range(N_BLOCKS):
+                nc.tensor.matmul(sqd[p][b][:], w_sq[:, b * P : (b + 1) * P], ones_mv[:], start=True, stop=False)
+
+        rx = []
+        for p in range(N_PIECES):
+            piece = offsets[:, p * (PIECE // 16) : (p + 1) * (PIECE // 16)]
+            xg = picked.tile([P, PIECE], F32, name="xg", tag="picked")
+            nc.tensor.matmul(xg[:], ident[:], table_sb[:].indirect(piece), start=True, stop=True)
+            x_sq = work.tile([P, PIECE], BF16, name=f"x_sq{p}")
+            nc.scalar.activation(x_sq[:], xg[:], ACT.Square)
+            nc.tensor.matmul(e_ps[p][:], minus_ones_w[:], x_sq[:], start=False, stop=True)
+            for b in range(N_BLOCKS):
+                nc.tensor.matmul(
+                    sqd[p][b][:], w_m2[:, b * P : (b + 1) * P], table_sb[:].indirect(piece), start=False, stop=False
+                )
+                nc.tensor.matmul(sqd[p][b][:], ones_w[:], x_sq[:], start=False, stop=True)
+            rx_p = work.tile([P, PIECE], F32, name=f"rx{p}")
+            nc.vector.reciprocal(rx_p[:], e_ps[p][:])
+            rx.append(rx_p)
+
+        tiles = [(p, b) for p in range(N_PIECES) for b in range(N_BLOCKS)]
+        t_of, root_of = {}, {}
+        for p, b in tiles:
+            t = work.tile([P, PIECE], F32, name=f"t{p}{b}")
+            nc.vector.scalar_tensor_tensor(t[:], sqd[p][b][:], TINY, rx[p][:], op0=ALU.max, op1=ALU.mult)
+            tt = work.tile([P, PIECE], F32, name=f"tt{p}{b}")
+            nc.vector.scalar_tensor_tensor(tt[:], t[:], f[:, b : b + 1], t[:], op0=ALU.add, op1=ALU.mult)
+            root = work.tile([P, PIECE], F32, name=f"root{p}{b}")
+            nc.scalar.activation(root[:], tt[:], ACT.Sqrt)
+            t_of[p, b], root_of[p, b] = t, root
+        for p, b in tiles:
+            y = work.tile([P, PIECE], F32, name=f"y{p}{b}")
+            nc.vector.tensor_tensor(y[:], t_of[p, b][:], root_of[p, b][:], ALU.add)
+            dist = work.tile([P, PIECE], F32, name=f"dist{p}{b}")
+            nc.scalar.activation(dist[:], y[:], ACT.Ln, bias=1.0, scale=s[:, b : b + 1])
+            nc.sync.dma_start(out[b * P : (b + 1) * P, p * PIECE : (p + 1) * PIECE], dist[:])

@@ -8,7 +8,6 @@ KEPT = 1024
 PIECE = 512
 N_PIECES = KEPT // PIECE
 N_BLOCKS = CENTROIDS // P
-TINY = 1e-30
 
 FLOPS = 2 * P * CENTROIDS * KEPT + 2 * P * KEPT + 2 * P * CENTROIDS
 BYTES = 2 * P * KEPT + 2 * P * CENTROIDS + 2 * P * (KEPT // 16) + 4 * CENTROIDS * KEPT
@@ -39,66 +38,61 @@ def tile_centroiddistance_kernel(tc, table, w, offs, out):
         make_identity(nc, ident[:])
         ones_w = held.tile([P, P], BF16, name="ones_w")
         nc.vector.memset(ones_w[:], 1.0)
-        minus_ones_w = held.tile([P, P], BF16, name="minus_ones_w")
-        nc.vector.memset(minus_ones_w[:], -1.0)
-        ones_mv = held.tile([P, PIECE], BF16, name="ones_mv")
-        nc.gpsimd.memset(ones_mv[:], 1.0)
-        inv_p_mv = held.tile([P, PIECE], BF16, name="inv_p_mv")
-        nc.gpsimd.memset(inv_p_mv[:], 1.0 / P)
 
         w_sq = held.tile([P, CENTROIDS], BF16, name="w_sq")
         nc.vector.tensor_tensor(w_sq[:], w_sb[:], w_sb[:], ALU.mult)
         w_m2 = held.tile([P, CENTROIDS], BF16, name="w_m2")
         nc.vector.tensor_scalar(w_m2[:], w_sb[:], -2.0, None, op0=ALU.mult)
-
         c2_ps = picked.tile([P, N_BLOCKS], F32, name="c2_ps", tag="picked")
         for b in range(N_BLOCKS):
-            nc.tensor.matmul(
-                c2_ps[:, b : b + 1], w_sq[:, b * P : (b + 1) * P], ones_mv[:, 0:1], start=True, stop=True
-            )
+            nc.tensor.matmul(c2_ps[:, b : b + 1], w_sq[:, b * P : (b + 1) * P], ones_w[:, 0:1], start=True, stop=True)
         f = held.tile([P, N_BLOCKS], F32, name="f")
         nc.vector.tensor_scalar(f[:], c2_ps[:], -1.0, 1.0, op0=ALU.mult, op1=ALU.add)
-        s = held.tile([P, N_BLOCKS], F32, name="s")
-        nc.vector.reciprocal(s[:], f[:])
-        nc.vector.tensor_scalar(s[:], s[:], 2.0, None, op0=ALU.mult)
+        rf = held.tile([P, N_BLOCKS], F32, name="rf")
+        nc.vector.reciprocal(rf[:], f[:])
+        c2_rf = held.tile([P, N_BLOCKS], F32, name="c2_rf")
+        nc.vector.tensor_scalar(c2_rf[:], rf[:], -1.0, None, op0=ALU.add)
 
-        sqd = [[sums.tile([P, PIECE], F32, name=f"sqd{p}{b}") for b in range(N_BLOCKS)] for p in range(N_PIECES)]
-        e_ps = [sums.tile([P, PIECE], F32, name=f"e_ps{p}") for p in range(N_PIECES)]
+        pieces = [offsets[:, p * (PIECE // 16) : (p + 1) * (PIECE // 16)] for p in range(N_PIECES)]
+        x_sq, e = [], []
         for p in range(N_PIECES):
-            nc.tensor.matmul(e_ps[p][:], ones_w[:], inv_p_mv[:], start=True, stop=False)
-            for b in range(N_BLOCKS):
-                nc.tensor.matmul(sqd[p][b][:], w_sq[:, b * P : (b + 1) * P], ones_mv[:], start=True, stop=False)
-
-        rx = []
-        for p in range(N_PIECES):
-            piece = offsets[:, p * (PIECE // 16) : (p + 1) * (PIECE // 16)]
             xg = picked.tile([P, PIECE], F32, name="xg", tag="picked")
-            nc.tensor.matmul(xg[:], ident[:], table_sb[:].indirect(piece), start=True, stop=True)
-            x_sq = work.tile([P, PIECE], BF16, name=f"x_sq{p}")
-            nc.scalar.activation(x_sq[:], xg[:], ACT.Square)
-            nc.tensor.matmul(e_ps[p][:], minus_ones_w[:], x_sq[:], start=False, stop=True)
+            nc.tensor.matmul(xg[:], ident[:], table_sb[:].indirect(pieces[p]), start=True, stop=True)
+            x_sq_p = work.tile([P, PIECE], BF16, name=f"x_sq{p}")
+            nc.scalar.activation(x_sq_p[:], xg[:], ACT.Square)
+            x_sq.append(x_sq_p)
+        part = [[sums.tile([P, PIECE], F32, name=f"part{p}{b}") for b in range(N_BLOCKS)] for p in range(N_PIECES)]
+        for p in range(N_PIECES):
             for b in range(N_BLOCKS):
                 nc.tensor.matmul(
-                    sqd[p][b][:], w_m2[:, b * P : (b + 1) * P], table_sb[:].indirect(piece), start=False, stop=False
+                    part[p][b][:], w_m2[:, b * P : (b + 1) * P], table_sb[:].indirect(pieces[p]), start=True, stop=False
                 )
-                nc.tensor.matmul(sqd[p][b][:], ones_w[:], x_sq[:], start=False, stop=True)
-            rx_p = work.tile([P, PIECE], F32, name=f"rx{p}")
-            nc.vector.reciprocal(rx_p[:], e_ps[p][:])
-            rx.append(rx_p)
+            x2_ps = sums.tile([P, PIECE], F32, name=f"x2_ps{p}")
+            nc.tensor.matmul(x2_ps[:], ones_w[:], x_sq[p][:], start=True, stop=True)
+            for b in range(N_BLOCKS):
+                nc.tensor.matmul(part[p][b][:], ones_w[:], x_sq[p][:], start=False, stop=True)
+            e_p = work.tile([P, PIECE], F32, name=f"e{p}")
+            nc.vector.tensor_scalar(e_p[:], x2_ps[:], -1.0, 1.0, op0=ALU.mult, op1=ALU.add)
+            e.append(e_p)
 
         tiles = [(p, b) for p in range(N_PIECES) for b in range(N_BLOCKS)]
-        t_of, root_of = {}, {}
+        root_v, root_ve = {}, {}
         for p, b in tiles:
-            t = work.tile([P, PIECE], F32, name=f"t{p}{b}")
-            nc.vector.scalar_tensor_tensor(t[:], sqd[p][b][:], TINY, rx[p][:], op0=ALU.max, op1=ALU.mult)
-            tt = work.tile([P, PIECE], F32, name=f"tt{p}{b}")
-            nc.vector.scalar_tensor_tensor(tt[:], t[:], f[:, b : b + 1], t[:], op0=ALU.add, op1=ALU.mult)
-            root = work.tile([P, PIECE], F32, name=f"root{p}{b}")
-            nc.scalar.activation(root[:], tt[:], ACT.Sqrt)
-            t_of[p, b], root_of[p, b] = t, root
-        for p, b in tiles:
-            y = work.tile([P, PIECE], F32, name=f"y{p}{b}")
-            nc.vector.tensor_tensor(y[:], t_of[p, b][:], root_of[p, b][:], ALU.add)
-            dist = work.tile([P, PIECE], F32, name=f"dist{p}{b}")
-            nc.scalar.activation(dist[:], y[:], ACT.Ln, bias=1.0, scale=s[:, b : b + 1])
-            nc.sync.dma_start(out[b * P : (b + 1) * P, p * PIECE : (p + 1) * PIECE], dist[:])
+            rf_b, c2_rf_b = rf[:, b : b + 1], c2_rf[:, b : b + 1]
+            root_v[p, b] = work.tile([P, PIECE], F32, name=f"root_v{p}{b}")
+            nc.scalar.activation(root_v[p, b][:], part[p][b][:], ACT.Sqrt, bias=c2_rf_b, scale=rf_b)
+            pe = work.tile([P, PIECE], F32, name=f"pe{p}{b}")
+            nc.vector.scalar_tensor_tensor(pe[:], part[p][b][:], rf_b, e[p][:], op0=ALU.mult, op1=ALU.add)
+            root_ve[p, b] = work.tile([P, PIECE], F32, name=f"root_ve{p}{b}")
+            nc.scalar.activation(root_ve[p, b][:], pe[:], ACT.Sqrt, bias=c2_rf_b)
+        for p in range(N_PIECES):
+            ln_e = work.tile([P, PIECE], F32, name=f"ln_e{p}")
+            nc.scalar.activation(ln_e[:], e[p][:], ACT.Ln)
+            for b in range(N_BLOCKS):
+                both = work.tile([P, PIECE], F32, name=f"both{p}{b}")
+                nc.vector.tensor_tensor(both[:], root_v[p, b][:], root_ve[p, b][:], ALU.add)
+                ln_both = work.tile([P, PIECE], F32, name=f"ln_both{p}{b}")
+                nc.scalar.activation(ln_both[:], both[:], ACT.Ln)
+                dist = work.tile([P, PIECE], F32, name=f"dist{p}{b}")
+                nc.vector.scalar_tensor_tensor(dist[:], ln_both[:], 2.0, ln_e[:], op0=ALU.mult, op1=ALU.subtract)
+                nc.sync.dma_start(out[b * P : (b + 1) * P, p * PIECE : (p + 1) * PIECE], dist[:])

@@ -8,6 +8,7 @@ KEPT = 1024
 PIECE = 512
 N_PIECES = KEPT // PIECE
 N_BLOCKS = CENTROIDS // P
+N_WARM = 5
 
 FLOPS = 2 * P * CENTROIDS * KEPT + 2 * P * KEPT + 2 * P * CENTROIDS
 BYTES = 2 * P * KEPT + 2 * P * CENTROIDS + 2 * P * (KEPT // 16) + 4 * CENTROIDS * KEPT
@@ -34,15 +35,24 @@ def tile_centroiddistance_kernel(tc, table, w, offs, out):
         nc.sync.dma_start(table_sb[:, :half], table[:, :half])
         nc.scalar.dma_start(table_sb[:, half:], table[:, half:])
 
+        scratch = held.tile([P, 1], F32, name="scratch")
+        nc.vector.memset(scratch[:], 1.0)
+        nc.scalar.activation(scratch[:], scratch[:], ACT.Sqrt)
         ident = held.tile([P, P], BF16, name="ident")
         make_identity(nc, ident[:])
         ones_w = held.tile([P, P], BF16, name="ones_w")
         nc.vector.memset(ones_w[:], 1.0)
 
+        ones_mv = held.tile([P, PIECE], BF16, name="ones_mv")
+        nc.vector.memset(ones_mv[:], 1.0)
+        warm_ps = sums.tile([P, PIECE], F32, name="warm_ps", tag="x2_ps1")
+        for i in range(N_WARM):
+            nc.tensor.matmul(warm_ps[:], ones_w[:], ones_mv[:], start=True, stop=True)
+
         w_sq = held.tile([P, CENTROIDS], BF16, name="w_sq")
         nc.vector.tensor_tensor(w_sq[:], w_sb[:], w_sb[:], ALU.mult)
         w_m2 = held.tile([P, CENTROIDS], BF16, name="w_m2")
-        nc.vector.tensor_scalar(w_m2[:], w_sb[:], -2.0, None, op0=ALU.mult)
+        nc.gpsimd.tensor_scalar(w_m2[:], w_sb[:], -2.0, 1.0, op0=ALU.mult, op1=ALU.mult)
         c2_ps = picked.tile([P, N_BLOCKS], F32, name="c2_ps", tag="picked")
         for b in range(N_BLOCKS):
             nc.tensor.matmul(c2_ps[:, b : b + 1], w_sq[:, b * P : (b + 1) * P], ones_w[:, 0:1], start=True, stop=True)
@@ -67,6 +77,7 @@ def tile_centroiddistance_kernel(tc, table, w, offs, out):
                 nc.tensor.matmul(
                     part[p][b][:], w_m2[:, b * P : (b + 1) * P], table_sb[:].indirect(pieces[p]), start=True, stop=False
                 )
+        for p in range(N_PIECES):
             x2_ps = sums.tile([P, PIECE], F32, name=f"x2_ps{p}")
             nc.tensor.matmul(x2_ps[:], ones_w[:], x_sq[p][:], start=True, stop=True)
             for b in range(N_BLOCKS):
@@ -85,14 +96,16 @@ def tile_centroiddistance_kernel(tc, table, w, offs, out):
             nc.vector.scalar_tensor_tensor(pe[:], part[p][b][:], rf_b, e[p][:], op0=ALU.mult, op1=ALU.add)
             root_ve[p, b] = work.tile([P, PIECE], F32, name=f"root_ve{p}{b}")
             nc.scalar.activation(root_ve[p, b][:], pe[:], ACT.Sqrt, bias=c2_rf_b)
+        zero = held.tile([P, 1], F32, name="zero")
+        nc.vector.tensor_scalar(zero[:], root_ve[tiles[-1]][:, 0:1], 0.0, 0.0, op0=ALU.min, op1=ALU.max)
         for p in range(N_PIECES):
             ln_e = work.tile([P, PIECE], F32, name=f"ln_e{p}")
-            nc.scalar.activation(ln_e[:], e[p][:], ACT.Ln)
+            nc.scalar.activation(ln_e[:], e[p][:], ACT.Ln, bias=zero[:])
             for b in range(N_BLOCKS):
                 both = work.tile([P, PIECE], F32, name=f"both{p}{b}")
                 nc.vector.tensor_tensor(both[:], root_v[p, b][:], root_ve[p, b][:], ALU.add)
                 ln_both = work.tile([P, PIECE], F32, name=f"ln_both{p}{b}")
-                nc.scalar.activation(ln_both[:], both[:], ACT.Ln)
+                nc.scalar.activation(ln_both[:], both[:], ACT.Ln, bias=zero[:])
                 dist = work.tile([P, PIECE], F32, name=f"dist{p}{b}")
                 nc.vector.scalar_tensor_tensor(dist[:], ln_both[:], 2.0, ln_e[:], op0=ALU.mult, op1=ALU.subtract)
                 nc.sync.dma_start(out[b * P : (b + 1) * P, p * PIECE : (p + 1) * PIECE], dist[:])

@@ -31,9 +31,10 @@ def tile_centroiddistance_kernel(tc, table, w, offs, out):
         w_sb = held.tile([P, CENTROIDS], BF16, name="w_sb")
         nc.scalar.dma_start(w_sb[:], w)
         table_sb = held.tile([P, STORE], BF16, name="table_sb")
-        half = STORE // 2
-        nc.sync.dma_start(table_sb[:, :half], table[:, :half])
-        nc.scalar.dma_start(table_sb[:, half:], table[:, half:])
+        quarter = STORE // 4
+        for q in range(4):
+            queue = nc.sync if q % 2 == 0 else nc.scalar
+            queue.dma_start(table_sb[:, q * quarter : (q + 1) * quarter], table[:, q * quarter : (q + 1) * quarter])
 
         scratch = held.tile([P, 1], F32, name="scratch")
         nc.vector.memset(scratch[:], 1.0)

@@ -6,6 +6,7 @@ STORE = 2048
 CENTROIDS = 256
 KEPT = 1024
 PIECE = 512
+HALF = PIECE // 2
 N_PIECES = KEPT // PIECE
 N_BLOCKS = CENTROIDS // P
 N_WARM = 5
@@ -31,10 +32,9 @@ def tile_centroiddistance_kernel(tc, table, w, offs, out):
         w_sb = held.tile([P, CENTROIDS], BF16, name="w_sb")
         nc.scalar.dma_start(w_sb[:], w)
         table_sb = held.tile([P, STORE], BF16, name="table_sb")
-        quarter = STORE // 4
-        for q in range(4):
-            queue = nc.sync if q % 2 == 0 else nc.scalar
-            queue.dma_start(table_sb[:, q * quarter : (q + 1) * quarter], table[:, q * quarter : (q + 1) * quarter])
+        half = STORE // 2
+        nc.sync.dma_start(table_sb[:, :half], table[:, :half])
+        nc.scalar.dma_start(table_sb[:, half:], table[:, half:])
 
         scratch = held.tile([P, 1], F32, name="scratch")
         nc.vector.memset(scratch[:], 1.0)
@@ -104,9 +104,16 @@ def tile_centroiddistance_kernel(tc, table, w, offs, out):
             nc.scalar.activation(ln_e[:], e[p][:], ACT.Ln, bias=zero[:])
             for b in range(N_BLOCKS):
                 both = work.tile([P, PIECE], F32, name=f"both{p}{b}")
-                nc.vector.tensor_tensor(both[:], root_v[p, b][:], root_ve[p, b][:], ALU.add)
+                nc.vector.scalar_tensor_tensor(
+                    both[:], root_v[p, b][:], 0.0, root_ve[p, b][:], op0=ALU.max, op1=ALU.add
+                )
                 ln_both = work.tile([P, PIECE], F32, name=f"ln_both{p}{b}")
-                nc.scalar.activation(ln_both[:], both[:], ACT.Ln, bias=zero[:])
                 dist = work.tile([P, PIECE], F32, name=f"dist{p}{b}")
-                nc.vector.scalar_tensor_tensor(dist[:], ln_both[:], 2.0, ln_e[:], op0=ALU.mult, op1=ALU.subtract)
-                nc.sync.dma_start(out[b * P : (b + 1) * P, p * PIECE : (p + 1) * PIECE], dist[:])
+                for h in range(2):
+                    cols = slice(h * HALF, (h + 1) * HALF)
+                    nc.scalar.activation(ln_both[:, cols], both[:, cols], ACT.Ln, bias=zero[:])
+                    nc.vector.scalar_tensor_tensor(
+                        dist[:, cols], ln_both[:, cols], 2.0, ln_e[:, cols], op0=ALU.mult, op1=ALU.subtract
+                    )
+                    first = p * PIECE + h * HALF
+                    nc.sync.dma_start(out[b * P : (b + 1) * P, first : first + HALF], dist[:, cols])

@@ -9,7 +9,6 @@ PIECE = 512
 HALF = PIECE // 2
 N_PIECES = KEPT // PIECE
 N_BLOCKS = CENTROIDS // P
-N_WARM = 5
 
 FLOPS = 2 * P * CENTROIDS * KEPT + 2 * P * KEPT + 2 * P * CENTROIDS
 BYTES = 2 * P * KEPT + 2 * P * CENTROIDS + 2 * P * (KEPT // 16) + 4 * CENTROIDS * KEPT
@@ -43,12 +42,6 @@ def tile_centroiddistance_kernel(tc, table, w, offs, out):
         make_identity(nc, ident[:])
         ones_w = held.tile([P, P], BF16, name="ones_w")
         nc.vector.memset(ones_w[:], 1.0)
-
-        ones_mv = held.tile([P, PIECE], BF16, name="ones_mv")
-        nc.vector.memset(ones_mv[:], 1.0)
-        warm_ps = sums.tile([P, PIECE], F32, name="warm_ps", tag="x2_ps1")
-        for i in range(N_WARM):
-            nc.tensor.matmul(warm_ps[:], ones_w[:], ones_mv[:], start=True, stop=True)
 
         w_sq = held.tile([P, CENTROIDS], BF16, name="w_sq")
         nc.vector.tensor_tensor(w_sq[:], w_sb[:], w_sb[:], ALU.mult)

@@ -42,6 +42,8 @@ def tile_centroiddistance_kernel(tc, table, w, offs, out):
         make_identity(nc, ident[:])
         ones_w = held.tile([P, P], BF16, name="ones_w")
         nc.vector.memset(ones_w[:], 1.0)
+        ident_f32 = held.tile([P, P], F32, name="ident_f32")
+        make_identity(nc, ident_f32[:])
 
         w_sq = held.tile([P, CENTROIDS], BF16, name="w_sq")
         nc.vector.tensor_tensor(w_sq[:], w_sb[:], w_sb[:], ALU.mult)
@@ -80,6 +82,27 @@ def tile_centroiddistance_kernel(tc, table, w, offs, out):
             nc.vector.tensor_scalar(e_p[:], x2_ps[:], -1.0, 1.0, op0=ALU.mult, op1=ALU.add)
             e.append(e_p)
 
+        chunks = KEPT // P
+        x2_col = picked.tile([P, chunks], F32, name="x2_col", tag="picked")
+        for c in range(chunks):
+            p, k = divmod(c * P, PIECE)
+            nc.tensor.matmul(x2_col[:, c : c + 1], x_sq[p][:, k : k + P], ones_w[:, 0:1], start=True, stop=True)
+        e_col = held.tile([P, chunks], F32, name="e_col")
+        nc.vector.tensor_scalar(e_col[:], x2_col[:], -1.0, 1.0, op0=ALU.mult, op1=ALU.add)
+        re_col = held.tile([P, chunks], F32, name="re_col")
+        nc.vector.reciprocal(re_col[:], e_col[:])
+        rho_col = held.tile([P, chunks], F32, name="rho_col")
+        nc.scalar.activation(rho_col[:], re_col[:], ACT.Sqrt)
+        rho = []
+        for p in range(N_PIECES):
+            rho_p = picked.tile([P, PIECE], F32, name="rho_p", tag="picked")
+            for k in range(0, PIECE, P):
+                c = (p * PIECE + k) // P
+                nc.tensor.matmul(
+                    rho_p[:, k : k + P], rho_col[:, c : c + 1].to_broadcast([P, P]), ident_f32[:], start=True, stop=True
+                )
+            rho.append(rho_p)
+
         tiles = [(p, b) for p in range(N_PIECES) for b in range(N_BLOCKS)]
         root_v, root_ve = {}, {}
         for p, b in tiles:
@@ -92,21 +115,20 @@ def tile_centroiddistance_kernel(tc, table, w, offs, out):
             nc.scalar.activation(root_ve[p, b][:], pe[:], ACT.Sqrt, bias=c2_rf_b)
         zero = held.tile([P, 1], F32, name="zero")
         nc.vector.tensor_scalar(zero[:], root_ve[tiles[-1]][:, 0:1], 0.0, 0.0, op0=ALU.min, op1=ALU.max)
-        for p in range(N_PIECES):
-            ln_e = work.tile([P, PIECE], F32, name=f"ln_e{p}")
-            nc.scalar.activation(ln_e[:], e[p][:], ACT.Ln, bias=zero[:])
-            for b in range(N_BLOCKS):
-                both = work.tile([P, PIECE], F32, name=f"both{p}{b}")
-                nc.vector.scalar_tensor_tensor(
-                    both[:], root_v[p, b][:], 0.0, root_ve[p, b][:], op0=ALU.max, op1=ALU.add
-                )
-                ln_both = work.tile([P, PIECE], F32, name=f"ln_both{p}{b}")
-                dist = work.tile([P, PIECE], F32, name=f"dist{p}{b}")
-                for h in range(2):
-                    cols = slice(h * HALF, (h + 1) * HALF)
-                    nc.scalar.activation(ln_both[:, cols], both[:, cols], ACT.Ln, bias=zero[:])
-                    nc.vector.scalar_tensor_tensor(
-                        dist[:, cols], ln_both[:, cols], 2.0, ln_e[:, cols], op0=ALU.mult, op1=ALU.subtract
-                    )
-                    first = p * PIECE + h * HALF
-                    nc.sync.dma_start(out[b * P : (b + 1) * P, first : first + HALF], dist[:, cols])
+        both = {}
+        for p, b in tiles:
+            both[p, b] = work.tile([P, PIECE], F32, name=f"both{p}{b}")
+            nc.vector.scalar_tensor_tensor(
+                both[p, b][:], root_v[p, b][:], 0.0, root_ve[p, b][:], op0=ALU.max, op1=ALU.add
+            )
+        for p, b in tiles:
+            scaled = work.tile([P, PIECE], F32, name=f"scaled{p}{b}")
+            nc.vector.tensor_tensor(scaled[:], both[p, b][:], rho[p][:], ALU.mult)
+            ln_both = work.tile([P, PIECE], F32, name=f"ln_both{p}{b}")
+            dist = work.tile([P, PIECE], F32, name=f"dist{p}{b}")
+            for h in range(2):
+                cols = slice(h * HALF, (h + 1) * HALF)
+                nc.scalar.activation(ln_both[:, cols], scaled[:, cols], ACT.Ln, bias=zero[:])
+                nc.vector.tensor_scalar(dist[:, cols], ln_both[:, cols], 2.0, None, op0=ALU.mult)
+                first = p * PIECE + h * HALF
+                nc.sync.dma_start(out[b * P : (b + 1) * P, first : first + HALF], dist[:, cols])

@@ -68,25 +68,62 @@ def tile_centroiddistance_kernel(tc, table, w, offs, out):
             nc.scalar.activation(x_sq_p[:], xg[:], ACT.Square)
             x_sq.append(x_sq_p)
         part = [[sums.tile([P, PIECE], F32, name=f"part{p}{b}") for b in range(N_BLOCKS)] for p in range(N_PIECES)]
-        for p in range(N_PIECES):
-            for b in range(N_BLOCKS):
-                nc.tensor.matmul(
-                    part[p][b][:], w_m2[:, b * P : (b + 1) * P], table_sb[:].indirect(pieces[p]), start=True, stop=False
-                )
-        for p in range(N_PIECES):
-            x2_ps = sums.tile([P, PIECE], F32, name=f"x2_ps{p}")
-            nc.tensor.matmul(x2_ps[:], ones_w[:], x_sq[p][:], start=True, stop=True)
-            for b in range(N_BLOCKS):
-                nc.tensor.matmul(part[p][b][:], ones_w[:], x_sq[p][:], start=False, stop=True)
+        x2_ps = [sums.tile([P, PIECE], F32, name=f"x2_ps{p}") for p in range(N_PIECES)]
+        chunk_cols = [slice(k, k + P) for k in range(0, PIECE, P)]
+
+        def xc_look_up(p, b, opens):
+            nc.tensor.matmul(
+                part[p][b][:],
+                w_m2[:, b * P : (b + 1) * P],
+                table_sb[:].indirect(pieces[p]),
+                start=opens,
+                stop=not opens,
+            )
+
+        def rows_of_x2(p):
+            for cols in chunk_cols:
+                nc.tensor.matmul(x2_ps[p][:, cols], ones_w[:], x_sq[p][:, cols], start=True, stop=True)
             e_p = work.tile([P, PIECE], F32, name=f"e{p}")
-            nc.vector.tensor_scalar(e_p[:], x2_ps[:], -1.0, 1.0, op0=ALU.mult, op1=ALU.add)
+            nc.vector.tensor_scalar(e_p[:], x2_ps[p][:], -1.0, 1.0, op0=ALU.mult, op1=ALU.add)
             e.append(e_p)
 
+        root_v, root_ve = {}, {}
+
+        def square_roots(p):
+            for b in range(N_BLOCKS):
+                root_v[p, b] = work.tile([P, PIECE], F32, name=f"root_v{p}{b}")
+                nc.scalar.activation(
+                    root_v[p, b][:], part[p][b][:], ACT.Sqrt, bias=c2_rf[:, b : b + 1], scale=rf[:, b : b + 1]
+                )
+            for b in range(N_BLOCKS):
+                pe = work.tile([P, PIECE], F32, name=f"pe{p}{b}")
+                nc.vector.scalar_tensor_tensor(
+                    pe[:], part[p][b][:], rf[:, b : b + 1], e[p][:], op0=ALU.mult, op1=ALU.add
+                )
+                root_ve[p, b] = work.tile([P, PIECE], F32, name=f"root_ve{p}{b}")
+                nc.scalar.activation(root_ve[p, b][:], pe[:], ACT.Sqrt, bias=c2_rf[:, b : b + 1])
+
+        for b in range(N_BLOCKS):
+            xc_look_up(0, b, opens=True)
+        rows_of_x2(0)
+        for b in range(N_BLOCKS):
+            for cols in chunk_cols:
+                nc.tensor.matmul(
+                    part[0][b][:, cols], ones_w[:], x_sq[0][:, cols], start=False, stop=cols is chunk_cols[-1]
+                )
         chunks = KEPT // P
         x2_col = picked.tile([P, chunks], F32, name="x2_col", tag="picked")
         for c in range(chunks):
             p, k = divmod(c * P, PIECE)
             nc.tensor.matmul(x2_col[:, c : c + 1], x_sq[p][:, k : k + P], ones_w[:, 0:1], start=True, stop=True)
+        square_roots(0)
+        rows_of_x2(1)
+        for b in range(N_BLOCKS):
+            nc.tensor.matmul(part[1][b][:], ones_w[:], x_sq[1][:], start=True, stop=False)
+        for b in range(N_BLOCKS):
+            xc_look_up(1, b, opens=False)
+        square_roots(1)
+
         e_col = held.tile([P, chunks], F32, name="e_col")
         nc.vector.tensor_scalar(e_col[:], x2_col[:], -1.0, 1.0, op0=ALU.mult, op1=ALU.add)
         re_col = held.tile([P, chunks], F32, name="re_col")
@@ -104,15 +141,6 @@ def tile_centroiddistance_kernel(tc, table, w, offs, out):
             rho.append(rho_p)
 
         tiles = [(p, b) for p in range(N_PIECES) for b in range(N_BLOCKS)]
-        root_v, root_ve = {}, {}
-        for p, b in tiles:
-            rf_b, c2_rf_b = rf[:, b : b + 1], c2_rf[:, b : b + 1]
-            root_v[p, b] = work.tile([P, PIECE], F32, name=f"root_v{p}{b}")
-            nc.scalar.activation(root_v[p, b][:], part[p][b][:], ACT.Sqrt, bias=c2_rf_b, scale=rf_b)
-            pe = work.tile([P, PIECE], F32, name=f"pe{p}{b}")
-            nc.vector.scalar_tensor_tensor(pe[:], part[p][b][:], rf_b, e[p][:], op0=ALU.mult, op1=ALU.add)
-            root_ve[p, b] = work.tile([P, PIECE], F32, name=f"root_ve{p}{b}")
-            nc.scalar.activation(root_ve[p, b][:], pe[:], ACT.Sqrt, bias=c2_rf_b)
         zero = held.tile([P, 1], F32, name="zero")
         nc.vector.tensor_scalar(zero[:], root_ve[tiles[-1]][:, 0:1], 0.0, 0.0, op0=ALU.min, op1=ALU.max)
         both = {}

import concourse.mybir as mybir
from concourse.masks import make_identity

P = 128
STORE = 2048
CENTROIDS = 256
KEPT = 1024
PIECE = 512
HALF = PIECE // 2
N_PIECES = KEPT // PIECE
N_BLOCKS = CENTROIDS // P

FLOPS = 2 * P * CENTROIDS * KEPT + 2 * P * KEPT + 2 * P * CENTROIDS
BYTES = 2 * P * KEPT + 2 * P * CENTROIDS + 2 * P * (KEPT // 16) + 4 * CENTROIDS * KEPT

BF16, F32, U16 = mybir.dt.bfloat16, mybir.dt.float32, mybir.dt.uint16
ALU = mybir.AluOpType
ACT = mybir.ActivationFunctionType


def tile_centroiddistance_kernel(tc, table, w, offs, out):
    nc = tc.nc
    with (
        tc.tile_pool(name="held", bufs=1) as held,
        tc.tile_pool(name="work", bufs=1) as work,
        tc.psum_pool(name="sums", bufs=1) as sums,
        tc.psum_pool(name="picked", bufs=2) as picked,
    ):
        offsets = held.tile([P, KEPT // 16], U16, name="offsets")
        nc.sync.dma_start(offsets[:], offs)
        w_sb = held.tile([P, CENTROIDS], BF16, name="w_sb")
        nc.scalar.dma_start(w_sb[:], w)
        table_sb = held.tile([P, STORE], BF16, name="table_sb")
        half = STORE // 2
        nc.sync.dma_start(table_sb[:, :half], table[:, :half])
        nc.scalar.dma_start(table_sb[:, half:], table[:, half:])

        scratch = held.tile([P, 1], F32, name="scratch")
        nc.vector.memset(scratch[:], 1.0)
        nc.scalar.activation(scratch[:], scratch[:], ACT.Sqrt)
        ident = held.tile([P, P], BF16, name="ident")
        make_identity(nc, ident[:])
        ones_w = held.tile([P, P], BF16, name="ones_w")
        nc.vector.memset(ones_w[:], 1.0)
        ident_f32 = held.tile([P, P], F32, name="ident_f32")
        make_identity(nc, ident_f32[:])

        w_sq = held.tile([P, CENTROIDS], BF16, name="w_sq")
        nc.vector.tensor_tensor(w_sq[:], w_sb[:], w_sb[:], ALU.mult)
        w_m2 = held.tile([P, CENTROIDS], BF16, name="w_m2")
        nc.gpsimd.tensor_scalar(w_m2[:], w_sb[:], -2.0, 1.0, op0=ALU.mult, op1=ALU.mult)
        c2_ps = picked.tile([P, N_BLOCKS], F32, name="c2_ps", tag="picked")
        for b in range(N_BLOCKS):
            nc.tensor.matmul(c2_ps[:, b : b + 1], w_sq[:, b * P : (b + 1) * P], ones_w[:, 0:1], start=True, stop=True)
        f = held.tile([P, N_BLOCKS], F32, name="f")
        nc.vector.tensor_scalar(f[:], c2_ps[:], -1.0, 1.0, op0=ALU.mult, op1=ALU.add)
        rf = held.tile([P, N_BLOCKS], F32, name="rf")
        nc.vector.reciprocal(rf[:], f[:])
        c2_rf = held.tile([P, N_BLOCKS], F32, name="c2_rf")
        nc.vector.tensor_scalar(c2_rf[:], rf[:], -1.0, None, op0=ALU.add)

        pieces = [offsets[:, p * (PIECE // 16) : (p + 1) * (PIECE // 16)] for p in range(N_PIECES)]
        x_sq, e = [], []
        for p in range(N_PIECES):
            xg = picked.tile([P, PIECE], F32, name="xg", tag="picked")
            nc.tensor.matmul(xg[:], ident[:], table_sb[:].indirect(pieces[p]), start=True, stop=True)
            x_sq_p = work.tile([P, PIECE], BF16, name=f"x_sq{p}")
            nc.scalar.activation(x_sq_p[:], xg[:], ACT.Square)
            x_sq.append(x_sq_p)
        part = [[sums.tile([P, PIECE], F32, name=f"part{p}{b}") for b in range(N_BLOCKS)] for p in range(N_PIECES)]
        x2_ps = [sums.tile([P, PIECE], F32, name=f"x2_ps{p}") for p in range(N_PIECES)]
        chunk_cols = [slice(k, k + P) for k in range(0, PIECE, P)]

        def xc_look_up(p, b, opens):
            nc.tensor.matmul(
                part[p][b][:],
                w_m2[:, b * P : (b + 1) * P],
                table_sb[:].indirect(pieces[p]),
                start=opens,
                stop=not opens,
            )

        def rows_of_x2(p):
            for cols in chunk_cols:
                nc.tensor.matmul(x2_ps[p][:, cols], ones_w[:], x_sq[p][:, cols], start=True, stop=True)
            e_p = work.tile([P, PIECE], F32, name=f"e{p}")
            nc.vector.tensor_scalar(e_p[:], x2_ps[p][:], -1.0, 1.0, op0=ALU.mult, op1=ALU.add)
            e.append(e_p)

        root_v, root_ve = {}, {}

        def square_roots(p):
            for b in range(N_BLOCKS):
                root_v[p, b] = work.tile([P, PIECE], F32, name=f"root_v{p}{b}")
                nc.scalar.activation(
                    root_v[p, b][:], part[p][b][:], ACT.Sqrt, bias=c2_rf[:, b : b + 1], scale=rf[:, b : b + 1]
                )
            for b in range(N_BLOCKS):
                pe = work.tile([P, PIECE], F32, name=f"pe{p}{b}")
                nc.vector.scalar_tensor_tensor(
                    pe[:], part[p][b][:], rf[:, b : b + 1], e[p][:], op0=ALU.mult, op1=ALU.add
                )
                root_ve[p, b] = work.tile([P, PIECE], F32, name=f"root_ve{p}{b}")
                nc.scalar.activation(root_ve[p, b][:], pe[:], ACT.Sqrt, bias=c2_rf[:, b : b + 1])

        for b in range(N_BLOCKS):
            xc_look_up(0, b, opens=True)
        rows_of_x2(0)
        for b in range(N_BLOCKS):
            for cols in chunk_cols:
                nc.tensor.matmul(
                    part[0][b][:, cols], ones_w[:], x_sq[0][:, cols], start=False, stop=cols is chunk_cols[-1]
                )
        chunks = KEPT // P
        x2_col = picked.tile([P, chunks], F32, name="x2_col", tag="picked")
        for c in range(chunks):
            p, k = divmod(c * P, PIECE)
            nc.tensor.matmul(x2_col[:, c : c + 1], x_sq[p][:, k : k + P], ones_w[:, 0:1], start=True, stop=True)
        square_roots(0)
        rows_of_x2(1)
        for b in range(N_BLOCKS):
            nc.tensor.matmul(part[1][b][:], ones_w[:], x_sq[1][:], start=True, stop=False)
        for b in range(N_BLOCKS):
            xc_look_up(1, b, opens=False)
        square_roots(1)

        e_col = held.tile([P, chunks], F32, name="e_col")
        nc.vector.tensor_scalar(e_col[:], x2_col[:], -1.0, 1.0, op0=ALU.mult, op1=ALU.add)
        re_col = held.tile([P, chunks], F32, name="re_col")
        nc.vector.reciprocal(re_col[:], e_col[:])
        rho_col = held.tile([P, chunks], F32, name="rho_col")
        nc.scalar.activation(rho_col[:], re_col[:], ACT.Sqrt)
        rho = []
        for p in range(N_PIECES):
            rho_p = picked.tile([P, PIECE], F32, name="rho_p", tag="picked")
            for k in range(0, PIECE, P):
                c = (p * PIECE + k) // P
                nc.tensor.matmul(
                    rho_p[:, k : k + P], rho_col[:, c : c + 1].to_broadcast([P, P]), ident_f32[:], start=True, stop=True
                )
            rho.append(rho_p)

        tiles = [(p, b) for p in range(N_PIECES) for b in range(N_BLOCKS)]
        zero = held.tile([P, 1], F32, name="zero")
        nc.vector.tensor_scalar(zero[:], root_ve[tiles[-1]][:, 0:1], 0.0, 0.0, op0=ALU.min, op1=ALU.max)
        both = {}
        for p, b in tiles:
            both[p, b] = work.tile([P, PIECE], F32, name=f"both{p}{b}")
            nc.vector.scalar_tensor_tensor(
                both[p, b][:], root_v[p, b][:], 0.0, root_ve[p, b][:], op0=ALU.max, op1=ALU.add
            )
        for p, b in tiles:
            scaled = work.tile([P, PIECE], F32, name=f"scaled{p}{b}")
            nc.vector.tensor_tensor(scaled[:], both[p, b][:], rho[p][:], ALU.mult)
            ln_both = work.tile([P, PIECE], F32, name=f"ln_both{p}{b}")
            dist = work.tile([P, PIECE], F32, name=f"dist{p}{b}")
            for h in range(2):
                cols = slice(h * HALF, (h + 1) * HALF)
                nc.scalar.activation(ln_both[:, cols], scaled[:, cols], ACT.Ln, bias=zero[:])
                nc.vector.tensor_scalar(dist[:, cols], ln_both[:, cols], 2.0, None, op0=ALU.mult)
                first = p * PIECE + h * HALF
                nc.sync.dma_start(out[b * P : (b + 1) * P, first : first + HALF], dist[:, cols])
